import numpy as np
import ml_dtypes


def mxq(x, axis, fmt="e4m3"):
    dtype, down = {"e4m3": (ml_dtypes.float8_e4m3fn, 7), "e5m2": (ml_dtypes.float8_e5m2, 14)}[fmt]
    v = np.moveaxis(np.asarray(x, np.float32).astype(ml_dtypes.bfloat16).astype(np.float64), axis, -1)
    blocks = v.reshape(v.shape[:-1] + (-1, 32))
    amax = np.abs(blocks).max(-1, keepdims=True)
    byte = np.maximum(np.where(amax > 0, np.frexp(amax)[1] - 1 + 127, 0) - down, 1)
    scale = np.exp2(byte - 127.0)
    codes = (blocks / scale).astype(np.float32).astype(dtype).astype(np.float64)
    return np.moveaxis((codes * scale).reshape(v.shape), -1, axis)


WIDE = False


def mx_kscale(k):
    if not WIDE:
        return np.ones(k)
    levels = np.array([10, -10, 5, -5, 0])
    a = np.random.permutation(np.resize(levels, k // 512 * 4)).reshape(k // 512, 4)
    idx = np.arange(k)
    return np.exp2(a[idx // 512, idx % 128 // 32])


BF16 = ml_dtypes.bfloat16


def bf(x):
    return np.asarray(x, np.float32).astype(BF16)


def f64(x):
    return np.asarray(x).astype(np.float64)


B, C_IN, C_OUT, H, W = 2, 1024, 768, 32, 32
P = 4
G = P * P


def setup_inputs():
    s = mx_kscale(C_IN)
    bound = np.sqrt(6.0 / (C_IN + C_OUT))
    return {"x": bf(np.random.standard_normal((B, C_IN, H, W)) * s[None, :, None, None]),
            "Wg": bf(np.random.uniform(-bound, bound, (G, C_OUT, C_IN)) / s[None, None, :]),
            "bg": bf(np.random.standard_normal((G, C_OUT)) * 0.25)}


def reference(x, Wg, bg):
    Bb, C, Hh, Ww = x.shape
    H4, W4 = Hh // P, Ww // P
    xq = mxq(f64(x), 1, "e4m3")
    wq = mxq(f64(Wg), 2, "e4m3")
    xg = xq.reshape(Bb, C, H4, P, W4, P).transpose(0, 2, 4, 3, 5, 1)
    xg = xg.reshape(Bb * H4 * W4, G, C).transpose(1, 0, 2)
    y = xg @ wq.transpose(0, 2, 1)
    O = y.shape[-1]
    y = y.transpose(1, 0, 2).reshape(Bb, H4, W4, G, O) + f64(bg)
    y = y.reshape(Bb, H4, W4, P, P, O).transpose(0, 5, 1, 3, 2, 4)
    return y.reshape(Bb, O, Hh, Ww)

@@ -1,0 +1,221 @@
+from contextlib import ExitStack
+
+import concourse.mybir as mybir
+from concourse.masks import make_identity
+
+F32 = mybir.dt.float32
+BF16 = mybir.dt.bfloat16
+U32 = mybir.dt.uint32
+U8 = mybir.dt.uint8
+FP8X4 = mybir.dt.float8_e4m3fn_x4
+
+FLOPS = 2 * 16 * 128 * 1024 * 768
+
+P = 128
+LOOK = 3
+RAW_BUFS = 8
+
+
+def tile_groupwiselinearprojector_kernel(tc, x, Wg, bg, out):
+    nc = tc.nc
+    with ExitStack() as ctx:
+        keep = ctx.enter_context(tc.tile_pool(name="keep", bufs=1))
+        rawp = ctx.enter_context(tc.tile_pool(name="rawp", bufs=RAW_BUFS))
+        grpp = ctx.enter_context(tc.tile_pool(name="grpp", bufs=5))
+        codp = ctx.enter_context(tc.tile_pool(name="codp", bufs=16))
+        tps = ctx.enter_context(tc.psum_pool(name="tps", bufs=6))
+        pos = ctx.enter_context(tc.psum_pool(name="pos", bufs=2))
+        ctx.enter_context(tc.manual_schedule())
+
+        ident = keep.tile([P, P], F32, name="ident")
+        make_identity(nc, ident[:])
+
+        bgpad = keep.tile([P, 768], BF16, name="bgpad")
+        nc.vector.memset(bgpad[:], 0.0)
+        nc.scalar.dma_start(out=bgpad[0:16, :], in_=bg)
+
+        chunks = ((0, 0), (1, 0), (0, 1), (1, 1))
+        xr = {}
+        for b, c in chunks:
+            t = rawp.tile([P, 6144], BF16, name="xr%d%d" % (b, c), tag="raw", align_bytes=64)
+            nc.sync.dma_start(
+                out=t[:, 0:4096].rearrange("p (u n) -> p u n", u=2),
+                in_=x[b, 512 * c : 512 * c + 512].rearrange("(u p e) h w -> p u (e h w)", u=2, p=P, e=2),
+            )
+            xr[(b, c)] = t
+
+        xc = keep.tile([P, 4096], U32, name="xc", align_bytes=64)
+        xs = keep.tile([P, 4096], U8, name="xs", align_bytes=64)
+        gx = {}
+        for c in range(2):
+            for gh in range(2):
+                gx[(c, gh)] = rawp.tile([P, 6144], BF16, name="gx%d%d" % (c, gh), tag="raw", align_bytes=64)
+
+        def regroup(b, c):
+            for pr in range(4):
+                src = (
+                    xr[(b, c)][:, 0:4096]
+                    .rearrange("p (a r n) -> p r a n", a=32, r=4, n=32)[:, pr]
+                    .rearrange("p (t h) (w q) -> p q h w t", t=4, q=4)
+                )
+                lo = (pr % 2) * 2048
+                dst = (
+                    gx[(c, pr // 2)][:, lo : lo + 2048]
+                    .rearrange("p (q b n) -> p q b n", q=4, b=2)[:, :, b]
+                    .rearrange("p q (h w t) -> p q h w t", h=8, w=8, t=4)
+                )
+                if pr < 3:
+                    nc.vector.tensor_copy(out=dst, in_=src)
+                else:
+                    for q in range(4):
+                        nc.scalar.copy(out=dst[:, q], in_=src[:, q])
+
+        def quant_x(c, gh):
+            base = (c * 16 + gh * 8) * P
+            nc.vector.quantize_mx(
+                out=xc[:, base : base + 1024].bitcast(FP8X4),
+                scales=xs[:, base : base + 1024],
+                in_=gx[(c, gh)][:, 0:4096],
+            )
+
+        regroup(0, 0)
+
+        regroup(1, 0)
+        regroup(0, 1)
+        quant_x(0, 0)
+        quant_x(0, 1)
+        regroup(1, 1)
+        quant_x(1, 0)
+        quant_x(1, 1)
+
+        bgf = keep.tile([P, 768], F32, name="bgf")
+        nc.vector.tensor_copy(
+            out=bgf[:].rearrange("g (j q) -> g j q", j=6),
+            in_=bgpad[:].rearrange("g (q j) -> g j q", j=6),
+        )
+
+        bias = keep.tile([P, 96], F32, name="bias")
+
+        def spread_bias():
+            for js in ((0, 1, 2, 3), (4, 5)):
+                tb = tps.tile([P, 512], F32, name="tb%d" % js[0], tag="tp")
+                for n, j in enumerate(js):
+                    nc.tensor.transpose(tb[:, n * P : (n + 1) * P], bgf[:, j * P : (j + 1) * P], ident[:])
+                nc.scalar.copy(
+                    out=bias[:, js[0] * 16 : (js[-1] + 1) * 16].rearrange("p (j g) -> p j g", g=16),
+                    in_=tb[:, 0 : len(js) * P].rearrange("p (j g) -> p j g", g=P)[:, :, 0:16],
+                )
+
+        ot = [keep.tile([P, 2048], F32, name="ot%d" % j) for j in range(6)]
+
+        pairs = []
+        last_pair = []
+        for g in range(12):
+            for jp in range(3):
+                pairs.append((g, ((g, 2 * jp, 2 * jp * 512), (g, 2 * jp + 1, (2 * jp + 1) * 512))))
+            last_pair.append(len(pairs) - 1)
+        for j in range(6):
+            for h in range(2):
+                pairs.append((12 + j, ((12 + 2 * h, j, 2 * h * 512), (13 + 2 * h, j, (2 * h + 1) * 512))))
+            last_pair.append(len(pairs) - 1)
+        n_pairs = len(pairs)
+        sched = [[] for k in range(n_pairs)]
+        for pr in range(3):
+            for j in range(6):
+                sched[12 * pr + 10 + j].append((pr, j))
+        for j in range(6):
+            sched[37 + 2 * j].append((3, j))
+
+        raw = {}
+
+        def load_w(m):
+            t = rawp.tile([P, 6144], BF16, name="wr%d" % m, tag="raw", align_bytes=64)
+            if m < 12:
+                nc.sync.dma_start(out=t[:], in_=Wg[m].rearrange("(q j) k -> q (j k)", j=6))
+            else:
+                nc.sync.dma_start(
+                    out=t[:, 0:4096].rearrange("p (g k) -> p g k", g=4),
+                    in_=Wg[12:16].rearrange("g (q j) k -> q g j k", j=6)[:, :, m - 12, :],
+                )
+            raw[m] = t
+
+        grp = {}
+        codes = {}
+
+        def transpose_pair(i):
+            m, units = pairs[i]
+            words = raw[m][:].bitcast(F32)
+            gt = grpp.tile([P, 2048], BF16, name="grp%d" % i, tag="grp", align_bytes=64)
+            g32 = gt[:].bitcast(F32)
+            banks = []
+            for n, (g, j, off) in enumerate(units):
+                tp = tps.tile([P, 512], F32, name="tp%d_%d" % (i, n), tag="tp")
+                for s in range(4):
+                    nc.tensor.transpose(tp[:, s * P : (s + 1) * P], words[:, off + s * P : off + (s + 1) * P], ident[:])
+                banks.append(tp)
+            for n, tp in enumerate(banks):
+                nc.scalar.copy(
+                    out=g32[:, n * 512 : (n + 1) * 512].rearrange("p (c o u) -> p c o u", c=2, o=P, u=2),
+                    in_=tp[:].rearrange("p (c u o) -> p c o u", c=2, u=2, o=P),
+                )
+            grp[i] = gt
+
+        def quant_pair(i):
+            wc = codp.tile([P, 512], U32, name="wc%d" % i, tag="wc", align_bytes=64)
+            ws = codp.tile([P, 512], U8, name="ws%d" % i, tag="ws", align_bytes=64)
+            nc.vector.quantize_mx(out=wc[:].bitcast(FP8X4), scales=ws[:], in_=grp[i][:])
+            for n, (g, j, off) in enumerate(pairs[i][1]):
+                codes[(g, j)] = (wc, ws, n)
+
+        def multiply(pr, j):
+            po = pos.tile([P, 512], F32, name="po%d_%d" % (pr, j), tag="po")
+            for q in range(4):
+                g = 4 * pr + q
+                wc, ws, n = codes[(g, j)]
+                for c in range(2):
+                    wl = (2 * n + c) * P
+                    xl = (16 * c + g) * P
+                    nc.tensor.matmul_mx(
+                        out=po[:, q * P : (q + 1) * P],
+                        lhsT=wc[:, wl : wl + P].bitcast(FP8X4),
+                        lhsT_scale=ws[:, wl : wl + P],
+                        rhs=xc[:, xl : xl + P].bitcast(FP8X4),
+                        rhs_scale=xs[:, xl : xl + P],
+                        start=(c == 0),
+                        stop=(c == 1),
+                    )
+            return po
+
+        def add_bias(pr, j, po):
+            lo = 16 * j + 4 * pr
+            nc.vector.tensor_tensor(
+                out=ot[j][:].rearrange("p (a r n) -> p r a n", a=16, r=4, n=32)[:, pr].rearrange("p a (w q) -> p a w q", q=4),
+                in0=po[:].rearrange("p (q a w) -> p a w q", q=4, a=16, w=8),
+                in1=bias[:, lo : lo + 4].unsqueeze(1).unsqueeze(1).to_broadcast([P, 16, 8, 4]),
+                op=mybir.AluOpType.add,
+            )
+            if pr == 3:
+                nc.sync.dma_start(
+                    out=out.rearrange("b (q j) h w -> j q b (h w)", j=6)[j],
+                    in_=ot[j][:].rearrange("p (b n) -> p b n", b=2),
+                )
+
+        next_m = 0
+        pending = []
+        for i in range(n_pairs + LOOK + 1):
+            while next_m < len(last_pair) and (next_m < RAW_BUFS or last_pair[next_m - RAW_BUFS] < i):
+                load_w(next_m)
+                next_m += 1
+            if i == 4:
+                spread_bias()
+            if i < n_pairs:
+                transpose_pair(i)
+            k = i - LOOK
+            if 0 <= k < n_pairs:
+                quant_pair(k)
+            for pr, j, po in pending:
+                add_bias(pr, j, po)
+            pending = []
+            if 0 <= k < n_pairs:
+                for pr, j in sched[k]:
+                    pending.append((pr, j, multiply(pr, j)))

@@ -14,6 +14,7 @@ FLOPS = 2 * 16 * 128 * 1024 * 768
 P = 128
 LOOK = 3
 RAW_BUFS = 8
+HEAD_TILES = 2
 
 
 def tile_groupwiselinearprojector_kernel(tc, x, Wg, bg, out):
@@ -34,6 +35,41 @@ def tile_groupwiselinearprojector_kernel(tc, x, Wg, bg, out):
         nc.vector.memset(bgpad[:], 0.0)
         nc.scalar.dma_start(out=bgpad[0:16, :], in_=bg)
 
+        tiles = [(g, 0, 6) for g in range(12)] + [(g, 0, 4) for g in range(12, 16)] + [(g, 4, 2) for g in range(12, 16)]
+        pairs = []
+        last_pair = []
+        where = {}
+        for m, (g, j0, nj) in enumerate(tiles):
+            for jj in range(0, nj, 2):
+                where[(g, j0 + jj)] = len(pairs)
+                where[(g, j0 + jj + 1)] = len(pairs)
+                pairs.append((m, ((g, j0 + jj, jj * 512), (g, j0 + jj + 1, (jj + 1) * 512))))
+            last_pair.append(len(pairs) - 1)
+        n_pairs = len(pairs)
+        sched = [[] for k in range(n_pairs)]
+        for pr in range(4):
+            for j in range(6):
+                ready = max([where[(4 * pr + q, j)] for q in range(4)])
+                if pr < 3:
+                    first = max([where[(4 * pr + q, 0)] for q in range(4)])
+                    sched[first + 1 + 2 * (j // 2)].append((pr, j))
+                else:
+                    sched[ready].append((pr, j))
+
+        raw = {}
+
+        def load_w(m):
+            g, j0, nj = tiles[m]
+            t = rawp.tile([P, 6144], BF16, name="wr%d" % m, tag="raw", align_bytes=64)
+            nc.sync.dma_start(
+                out=t[:, 0 : nj * 1024],
+                in_=Wg[g].rearrange("(q j) k -> q (j k)", j=6)[:, j0 * 1024 : (j0 + nj) * 1024],
+            )
+            raw[m] = t
+
+        for m in range(HEAD_TILES):
+            load_w(m)
+
         chunks = ((0, 0), (1, 0), (0, 1), (1, 1))
         xr = {}
         for b, c in chunks:
@@ -47,9 +83,6 @@ def tile_groupwiselinearprojector_kernel(tc, x, Wg, bg, out):
         xc = keep.tile([P, 4096], U32, name="xc", align_bytes=64)
         xs = keep.tile([P, 4096], U8, name="xs", align_bytes=64)
         gx = {}
-        for c in range(2):
-            for gh in range(2):
-                gx[(c, gh)] = rawp.tile([P, 6144], BF16, name="gx%d%d" % (c, gh), tag="raw", align_bytes=64)
 
         def regroup(b, c):
             for pr in range(4):
@@ -78,23 +111,25 @@ def tile_groupwiselinearprojector_kernel(tc, x, Wg, bg, out):
                 in_=gx[(c, gh)][:, 0:4096],
             )
 
-        regroup(0, 0)
-
-        regroup(1, 0)
-        regroup(0, 1)
-        quant_x(0, 0)
-        quant_x(0, 1)
-        regroup(1, 1)
-        quant_x(1, 0)
-        quant_x(1, 1)
-
         bgf = keep.tile([P, 768], F32, name="bgf")
-        nc.vector.tensor_copy(
-            out=bgf[:].rearrange("g (j q) -> g j q", j=6),
-            in_=bgpad[:].rearrange("g (q j) -> g j q", j=6),
-        )
-
         bias = keep.tile([P, 96], F32, name="bias")
+
+        def x_stage():
+            for c in range(2):
+                for gh in range(2):
+                    gx[(c, gh)] = rawp.tile([P, 6144], BF16, name="gx%d%d" % (c, gh), tag="raw", align_bytes=64)
+            regroup(0, 0)
+            regroup(1, 0)
+            regroup(0, 1)
+            quant_x(0, 0)
+            quant_x(0, 1)
+            regroup(1, 1)
+            quant_x(1, 0)
+            quant_x(1, 1)
+            nc.vector.tensor_copy(
+                out=bgf[:].rearrange("g (j q) -> g j q", j=6),
+                in_=bgpad[:].rearrange("g (q j) -> g j q", j=6),
+            )
 
         def spread_bias():
             for js in ((0, 1, 2, 3), (4, 5)):
@@ -107,38 +142,6 @@ def tile_groupwiselinearprojector_kernel(tc, x, Wg, bg, out):
                 )
 
         ot = [keep.tile([P, 2048], F32, name="ot%d" % j) for j in range(6)]
-
-        pairs = []
-        last_pair = []
-        for g in range(12):
-            for jp in range(3):
-                pairs.append((g, ((g, 2 * jp, 2 * jp * 512), (g, 2 * jp + 1, (2 * jp + 1) * 512))))
-            last_pair.append(len(pairs) - 1)
-        for j in range(6):
-            for h in range(2):
-                pairs.append((12 + j, ((12 + 2 * h, j, 2 * h * 512), (13 + 2 * h, j, (2 * h + 1) * 512))))
-            last_pair.append(len(pairs) - 1)
-        n_pairs = len(pairs)
-        sched = [[] for k in range(n_pairs)]
-        for pr in range(3):
-            for j in range(6):
-                sched[12 * pr + 10 + j].append((pr, j))
-        for j in range(6):
-            sched[37 + 2 * j].append((3, j))
-
-        raw = {}
-
-        def load_w(m):
-            t = rawp.tile([P, 6144], BF16, name="wr%d" % m, tag="raw", align_bytes=64)
-            if m < 12:
-                nc.sync.dma_start(out=t[:], in_=Wg[m].rearrange("(q j) k -> q (j k)", j=6))
-            else:
-                nc.sync.dma_start(
-                    out=t[:, 0:4096].rearrange("p (g k) -> p g k", g=4),
-                    in_=Wg[12:16].rearrange("g (q j) k -> q g j k", j=6)[:, :, m - 12, :],
-                )
-            raw[m] = t
-
         grp = {}
         codes = {}
 
@@ -200,19 +203,28 @@ def tile_groupwiselinearprojector_kernel(tc, x, Wg, bg, out):
                     in_=ot[j][:].rearrange("p (b n) -> p b n", b=2),
                 )
 
-        next_m = 0
+        head_pairs = last_pair[HEAD_TILES - 1] + 1
+        next_m = HEAD_TILES
+        next_q = 0
         pending = []
         for i in range(n_pairs + LOOK + 1):
-            while next_m < len(last_pair) and (next_m < RAW_BUFS or last_pair[next_m - RAW_BUFS] < i):
-                load_w(next_m)
-                next_m += 1
-            if i == 4:
+            if i == head_pairs:
+                while next_q < head_pairs:
+                    quant_pair(next_q)
+                    next_q += 1
+                x_stage()
+            if i >= head_pairs:
+                while next_m < len(tiles) and (next_m < RAW_BUFS + HEAD_TILES or last_pair[next_m - RAW_BUFS] < i):
+                    load_w(next_m)
+                    next_m += 1
+            if i == head_pairs + 4:
                 spread_bias()
             if i < n_pairs:
                 transpose_pair(i)
             k = i - LOOK
-            if 0 <= k < n_pairs:
+            if next_q <= k < n_pairs:
                 quant_pair(k)
+                next_q = k + 1
             for pr, j, po in pending:
                 add_bias(pr, j, po)
             pending = []

@@ -13,8 +13,8 @@ FLOPS = 2 * 16 * 128 * 1024 * 768
 
 P = 128
 LOOK = 3
-RAW_BUFS = 8
-HEAD_TILES = 2
+RAW_BUFS = 12
+PHASES = (4, 1, 1)
 
 
 def tile_groupwiselinearprojector_kernel(tc, x, Wg, bg, out):
@@ -35,45 +35,62 @@ def tile_groupwiselinearprojector_kernel(tc, x, Wg, bg, out):
         nc.vector.memset(bgpad[:], 0.0)
         nc.scalar.dma_start(out=bgpad[0:16, :], in_=bg)
 
-        tiles = [(g, 0, 6) for g in range(12)] + [(g, 0, 4) for g in range(12, 16)] + [(g, 4, 2) for g in range(12, 16)]
+        tiles = []
+        j0 = 0
+        for nj in PHASES:
+            if nj > 1:
+                for g in range(16):
+                    tiles.append([(g, j0 + a) for a in range(nj)])
+            else:
+                for g in range(0, 16, 2):
+                    tiles.append([(g, j0), (g + 1, j0)])
+            j0 += nj
         pairs = []
         last_pair = []
         where = {}
-        for m, (g, j0, nj) in enumerate(tiles):
-            for jj in range(0, nj, 2):
-                where[(g, j0 + jj)] = len(pairs)
-                where[(g, j0 + jj + 1)] = len(pairs)
-                pairs.append((m, ((g, j0 + jj, jj * 512), (g, j0 + jj + 1, (jj + 1) * 512))))
+        for m, units in enumerate(tiles):
+            for a in range(0, len(units), 2):
+                where[units[a]] = len(pairs)
+                where[units[a + 1]] = len(pairs)
+                pairs.append((m, ((units[a][0], units[a][1], a * 512), (units[a + 1][0], units[a + 1][1], (a + 1) * 512))))
             last_pair.append(len(pairs) - 1)
         n_pairs = len(pairs)
+        order = sorted([(max([where[(4 * pr + q, j)] for q in range(4)]), j, pr) for pr in range(4) for j in range(6)])
+        slots = []
+        for av, j, pr in order:
+            slots.append(max(av, slots[-1] + 2) if slots else av)
+        lim = n_pairs - 1
+        for n in reversed(range(len(order))):
+            if slots[n] > lim:
+                slots[n] = max(order[n][0], lim)
+            lim = min(lim, slots[n]) - 1
         sched = [[] for k in range(n_pairs)]
-        for pr in range(4):
-            for j in range(6):
-                ready = max([where[(4 * pr + q, j)] for q in range(4)])
-                if pr < 3:
-                    first = max([where[(4 * pr + q, 0)] for q in range(4)])
-                    sched[first + 1 + 2 * (j // 2)].append((pr, j))
-                else:
-                    sched[ready].append((pr, j))
+        for n, (av, j, pr) in enumerate(order):
+            sched[slots[n]].append((pr, j))
 
         raw = {}
 
         def load_w(m):
-            g, j0, nj = tiles[m]
-            t = rawp.tile([P, 6144], BF16, name="wr%d" % m, tag="raw", align_bytes=64)
-            nc.sync.dma_start(
-                out=t[:, 0 : nj * 1024],
-                in_=Wg[g].rearrange("(q j) k -> q (j k)", j=6)[:, j0 * 1024 : (j0 + nj) * 1024],
-            )
+            units = tiles[m]
+            t = rawp.tile([P, 4096], BF16, name="wr%d" % m, tag="raw", align_bytes=64)
+            g, j = units[0]
+            if units[1][0] == g:
+                nj = len(units)
+                nc.sync.dma_start(
+                    out=t[:, 0 : nj * 1024],
+                    in_=Wg[g].rearrange("(q j) k -> q (j k)", j=6)[:, j * 1024 : (j + nj) * 1024],
+                )
+            else:
+                nc.sync.dma_start(
+                    out=t[:, 0:2048].rearrange("p (g k) -> p g k", g=2),
+                    in_=Wg[g : g + 2].rearrange("g (q j) k -> q g j k", j=6)[:, :, j, :],
+                )
             raw[m] = t
-
-        for m in range(HEAD_TILES):
-            load_w(m)
 
         chunks = ((0, 0), (1, 0), (0, 1), (1, 1))
         xr = {}
         for b, c in chunks:
-            t = rawp.tile([P, 6144], BF16, name="xr%d%d" % (b, c), tag="raw", align_bytes=64)
+            t = rawp.tile([P, 4096], BF16, name="xr%d%d" % (b, c), tag="raw", align_bytes=64)
             nc.sync.dma_start(
                 out=t[:, 0:4096].rearrange("p (u n) -> p u n", u=2),
                 in_=x[b, 512 * c : 512 * c + 512].rearrange("(u p e) h w -> p u (e h w)", u=2, p=P, e=2),
@@ -117,7 +134,7 @@ def tile_groupwiselinearprojector_kernel(tc, x, Wg, bg, out):
         def x_stage():
             for c in range(2):
                 for gh in range(2):
-                    gx[(c, gh)] = rawp.tile([P, 6144], BF16, name="gx%d%d" % (c, gh), tag="raw", align_bytes=64)
+                    gx[(c, gh)] = rawp.tile([P, 4096], BF16, name="gx%d%d" % (c, gh), tag="raw", align_bytes=64)
             regroup(0, 0)
             regroup(1, 0)
             regroup(0, 1)
@@ -197,34 +214,28 @@ def tile_groupwiselinearprojector_kernel(tc, x, Wg, bg, out):
                 in1=bias[:, lo : lo + 4].unsqueeze(1).unsqueeze(1).to_broadcast([P, 16, 8, 4]),
                 op=mybir.AluOpType.add,
             )
-            if pr == 3:
+            done[j] += 1
+            if done[j] == 4:
                 nc.sync.dma_start(
                     out=out.rearrange("b (q j) h w -> j q b (h w)", j=6)[j],
                     in_=ot[j][:].rearrange("p (b n) -> p b n", b=2),
                 )
 
-        head_pairs = last_pair[HEAD_TILES - 1] + 1
-        next_m = HEAD_TILES
-        next_q = 0
+        done = [0] * 6
+        x_stage()
+        next_m = 0
         pending = []
         for i in range(n_pairs + LOOK + 1):
-            if i == head_pairs:
-                while next_q < head_pairs:
-                    quant_pair(next_q)
-                    next_q += 1
-                x_stage()
-            if i >= head_pairs:
-                while next_m < len(tiles) and (next_m < RAW_BUFS + HEAD_TILES or last_pair[next_m - RAW_BUFS] < i):
-                    load_w(next_m)
-                    next_m += 1
-            if i == head_pairs + 4:
+            while next_m < len(tiles) and (next_m < RAW_BUFS or last_pair[next_m - RAW_BUFS] < i):
+                load_w(next_m)
+                next_m += 1
+            if i == 8:
                 spread_bias()
             if i < n_pairs:
                 transpose_pair(i)
             k = i - LOOK
-            if next_q <= k < n_pairs:
+            if 0 <= k < n_pairs:
                 quant_pair(k)
-                next_q = k + 1
             for pr, j, po in pending:
                 add_bias(pr, j, po)
             pending = []

@@ -13,8 +13,9 @@ FLOPS = 2 * 16 * 128 * 1024 * 768
 
 P = 128
 LOOK = 3
-RAW_BUFS = 12
-PHASES = (4, 1, 1)
+RAW_BUFS = 9
+RAW_COLS = 5120
+PHASES = (5, 1)
 
 
 def tile_groupwiselinearprojector_kernel(tc, x, Wg, bg, out):
@@ -45,16 +46,15 @@ def tile_groupwiselinearprojector_kernel(tc, x, Wg, bg, out):
                 for g in range(0, 16, 2):
                     tiles.append([(g, j0), (g + 1, j0)])
             j0 += nj
-        pairs = []
-        last_pair = []
-        where = {}
-        for m, units in enumerate(tiles):
-            for a in range(0, len(units), 2):
-                where[units[a]] = len(pairs)
-                where[units[a + 1]] = len(pairs)
-                pairs.append((m, ((units[a][0], units[a][1], a * 512), (units[a + 1][0], units[a + 1][1], (a + 1) * 512))))
-            last_pair.append(len(pairs) - 1)
+        stream = [(m, g, j, a * 512) for m, units in enumerate(tiles) for a, (g, j) in enumerate(units)]
+        pairs = [(stream[n], stream[n + 1]) for n in range(0, len(stream), 2)]
         n_pairs = len(pairs)
+        where = {}
+        last_pair = [0] * len(tiles)
+        for i, units in enumerate(pairs):
+            for m, g, j, off in units:
+                where[(g, j)] = i
+                last_pair[m] = i
         order = sorted([(max([where[(4 * pr + q, j)] for q in range(4)]), j, pr) for pr in range(4) for j in range(6)])
         slots = []
         for av, j, pr in order:
@@ -72,7 +72,7 @@ def tile_groupwiselinearprojector_kernel(tc, x, Wg, bg, out):
 
         def load_w(m):
             units = tiles[m]
-            t = rawp.tile([P, 4096], BF16, name="wr%d" % m, tag="raw", align_bytes=64)
+            t = rawp.tile([P, RAW_COLS], BF16, name="wr%d" % m, tag="raw", align_bytes=64)
             g, j = units[0]
             if units[1][0] == g:
                 nj = len(units)
@@ -90,7 +90,7 @@ def tile_groupwiselinearprojector_kernel(tc, x, Wg, bg, out):
         chunks = ((0, 0), (1, 0), (0, 1), (1, 1))
         xr = {}
         for b, c in chunks:
-            t = rawp.tile([P, 4096], BF16, name="xr%d%d" % (b, c), tag="raw", align_bytes=64)
+            t = rawp.tile([P, RAW_COLS], BF16, name="xr%d%d" % (b, c), tag="raw", align_bytes=64)
             nc.sync.dma_start(
                 out=t[:, 0:4096].rearrange("p (u n) -> p u n", u=2),
                 in_=x[b, 512 * c : 512 * c + 512].rearrange("(u p e) h w -> p u (e h w)", u=2, p=P, e=2),
@@ -134,7 +134,7 @@ def tile_groupwiselinearprojector_kernel(tc, x, Wg, bg, out):
         def x_stage():
             for c in range(2):
                 for gh in range(2):
-                    gx[(c, gh)] = rawp.tile([P, 4096], BF16, name="gx%d%d" % (c, gh), tag="raw", align_bytes=64)
+                    gx[(c, gh)] = rawp.tile([P, RAW_COLS], BF16, name="gx%d%d" % (c, gh), tag="raw", align_bytes=64)
             regroup(0, 0)
             regroup(1, 0)
             regroup(0, 1)
@@ -163,12 +163,12 @@ def tile_groupwiselinearprojector_kernel(tc, x, Wg, bg, out):
         codes = {}
 
         def transpose_pair(i):
-            m, units = pairs[i]
-            words = raw[m][:].bitcast(F32)
+            units = pairs[i]
             gt = grpp.tile([P, 2048], BF16, name="grp%d" % i, tag="grp", align_bytes=64)
             g32 = gt[:].bitcast(F32)
             banks = []
-            for n, (g, j, off) in enumerate(units):
+            for n, (m, g, j, off) in enumerate(units):
+                words = raw[m][:].bitcast(F32)
                 tp = tps.tile([P, 512], F32, name="tp%d_%d" % (i, n), tag="tp")
                 for s in range(4):
                     nc.tensor.transpose(tp[:, s * P : (s + 1) * P], words[:, off + s * P : off + (s + 1) * P], ident[:])
@@ -184,7 +184,7 @@ def tile_groupwiselinearprojector_kernel(tc, x, Wg, bg, out):
             wc = codp.tile([P, 512], U32, name="wc%d" % i, tag="wc", align_bytes=64)
             ws = codp.tile([P, 512], U8, name="ws%d" % i, tag="ws", align_bytes=64)
             nc.vector.quantize_mx(out=wc[:].bitcast(FP8X4), scales=ws[:], in_=grp[i][:])
-            for n, (g, j, off) in enumerate(pairs[i][1]):
+            for n, (m, g, j, off) in enumerate(pairs[i]):
                 codes[(g, j)] = (wc, ws, n)
 
         def multiply(pr, j):

from contextlib import ExitStack

import concourse.mybir as mybir
from concourse.masks import make_identity

F32 = mybir.dt.float32
BF16 = mybir.dt.bfloat16
U32 = mybir.dt.uint32
U8 = mybir.dt.uint8
FP8X4 = mybir.dt.float8_e4m3fn_x4

FLOPS = 2 * 16 * 128 * 1024 * 768

P = 128
LOOK = 3
RAW_BUFS = 9
RAW_COLS = 5120
PHASES = (5, 1)


def tile_groupwiselinearprojector_kernel(tc, x, Wg, bg, out):
    nc = tc.nc
    with ExitStack() as ctx:
        keep = ctx.enter_context(tc.tile_pool(name="keep", bufs=1))
        rawp = ctx.enter_context(tc.tile_pool(name="rawp", bufs=RAW_BUFS))
        grpp = ctx.enter_context(tc.tile_pool(name="grpp", bufs=5))
        codp = ctx.enter_context(tc.tile_pool(name="codp", bufs=16))
        tps = ctx.enter_context(tc.psum_pool(name="tps", bufs=6))
        pos = ctx.enter_context(tc.psum_pool(name="pos", bufs=2))
        ctx.enter_context(tc.manual_schedule())

        ident = keep.tile([P, P], F32, name="ident")
        make_identity(nc, ident[:])

        bgpad = keep.tile([P, 768], BF16, name="bgpad")
        nc.vector.memset(bgpad[:], 0.0)
        nc.scalar.dma_start(out=bgpad[0:16, :], in_=bg)

        tiles = []
        j0 = 0
        for nj in PHASES:
            if nj > 1:
                for g in range(16):
                    tiles.append([(g, j0 + a) for a in range(nj)])
            else:
                for g in range(0, 16, 2):
                    tiles.append([(g, j0), (g + 1, j0)])
            j0 += nj
        stream = [(m, g, j, a * 512) for m, units in enumerate(tiles) for a, (g, j) in enumerate(units)]
        pairs = [(stream[n], stream[n + 1]) for n in range(0, len(stream), 2)]
        n_pairs = len(pairs)
        where = {}
        last_pair = [0] * len(tiles)
        for i, units in enumerate(pairs):
            for m, g, j, off in units:
                where[(g, j)] = i
                last_pair[m] = i
        order = sorted([(max([where[(4 * pr + q, j)] for q in range(4)]), j, pr) for pr in range(4) for j in range(6)])
        slots = []
        for av, j, pr in order:
            slots.append(max(av, slots[-1] + 2) if slots else av)
        lim = n_pairs - 1
        for n in reversed(range(len(order))):
            if slots[n] > lim:
                slots[n] = max(order[n][0], lim)
            lim = min(lim, slots[n]) - 1
        sched = [[] for k in range(n_pairs)]
        for n, (av, j, pr) in enumerate(order):
            sched[slots[n]].append((pr, j))

        raw = {}

        def load_w(m):
            units = tiles[m]
            t = rawp.tile([P, RAW_COLS], BF16, name="wr%d" % m, tag="raw", align_bytes=64)
            g, j = units[0]
            if units[1][0] == g:
                nj = len(units)
                nc.sync.dma_start(
                    out=t[:, 0 : nj * 1024],
                    in_=Wg[g].rearrange("(q j) k -> q (j k)", j=6)[:, j * 1024 : (j + nj) * 1024],
                )
            else:
                nc.sync.dma_start(
                    out=t[:, 0:2048].rearrange("p (g k) -> p g k", g=2),
                    in_=Wg[g : g + 2].rearrange("g (q j) k -> q g j k", j=6)[:, :, j, :],
                )
            raw[m] = t

        chunks = ((0, 0), (1, 0), (0, 1), (1, 1))
        xr = {}
        for b, c in chunks:
            t = rawp.tile([P, RAW_COLS], BF16, name="xr%d%d" % (b, c), tag="raw", align_bytes=64)
            nc.sync.dma_start(
                out=t[:, 0:4096].rearrange("p (u n) -> p u n", u=2),
                in_=x[b, 512 * c : 512 * c + 512].rearrange("(u p e) h w -> p u (e h w)", u=2, p=P, e=2),
            )
            xr[(b, c)] = t

        xc = keep.tile([P, 4096], U32, name="xc", align_bytes=64)
        xs = keep.tile([P, 4096], U8, name="xs", align_bytes=64)
        gx = {}

        def regroup(b, c):
            for pr in range(4):
                src = (
                    xr[(b, c)][:, 0:4096]
                    .rearrange("p (a r n) -> p r a n", a=32, r=4, n=32)[:, pr]
                    .rearrange("p (t h) (w q) -> p q h w t", t=4, q=4)
                )
                lo = (pr % 2) * 2048
                dst = (
                    gx[(c, pr // 2)][:, lo : lo + 2048]
                    .rearrange("p (q b n) -> p q b n", q=4, b=2)[:, :, b]
                    .rearrange("p q (h w t) -> p q h w t", h=8, w=8, t=4)
                )
                if pr < 3:
                    nc.vector.tensor_copy(out=dst, in_=src)
                else:
                    for q in range(4):
                        nc.scalar.copy(out=dst[:, q], in_=src[:, q])

        def quant_x(c, gh):
            base = (c * 16 + gh * 8) * P
            nc.vector.quantize_mx(
                out=xc[:, base : base + 1024].bitcast(FP8X4),
                scales=xs[:, base : base + 1024],
                in_=gx[(c, gh)][:, 0:4096],
            )

        bgf = keep.tile([P, 768], F32, name="bgf")
        bias = keep.tile([P, 96], F32, name="bias")

        def x_stage():
            for c in range(2):
                for gh in range(2):
                    gx[(c, gh)] = rawp.tile([P, RAW_COLS], BF16, name="gx%d%d" % (c, gh), tag="raw", align_bytes=64)
            regroup(0, 0)
            regroup(1, 0)
            regroup(0, 1)
            quant_x(0, 0)
            quant_x(0, 1)
            regroup(1, 1)
            quant_x(1, 0)
            quant_x(1, 1)
            nc.vector.tensor_copy(
                out=bgf[:].rearrange("g (j q) -> g j q", j=6),
                in_=bgpad[:].rearrange("g (q j) -> g j q", j=6),
            )

        def spread_bias():
            for js in ((0, 1, 2, 3), (4, 5)):
                tb = tps.tile([P, 512], F32, name="tb%d" % js[0], tag="tp")
                for n, j in enumerate(js):
                    nc.tensor.transpose(tb[:, n * P : (n + 1) * P], bgf[:, j * P : (j + 1) * P], ident[:])
                nc.scalar.copy(
                    out=bias[:, js[0] * 16 : (js[-1] + 1) * 16].rearrange("p (j g) -> p j g", g=16),
                    in_=tb[:, 0 : len(js) * P].rearrange("p (j g) -> p j g", g=P)[:, :, 0:16],
                )

        ot = [keep.tile([P, 2048], F32, name="ot%d" % j) for j in range(6)]
        grp = {}
        codes = {}

        def transpose_pair(i):
            units = pairs[i]
            gt = grpp.tile([P, 2048], BF16, name="grp%d" % i, tag="grp", align_bytes=64)
            g32 = gt[:].bitcast(F32)
            banks = []
            for n, (m, g, j, off) in enumerate(units):
                words = raw[m][:].bitcast(F32)
                tp = tps.tile([P, 512], F32, name="tp%d_%d" % (i, n), tag="tp")
                for s in range(4):
                    nc.tensor.transpose(tp[:, s * P : (s + 1) * P], words[:, off + s * P : off + (s + 1) * P], ident[:])
                banks.append(tp)
            for n, tp in enumerate(banks):
                nc.scalar.copy(
                    out=g32[:, n * 512 : (n + 1) * 512].rearrange("p (c o u) -> p c o u", c=2, o=P, u=2),
                    in_=tp[:].rearrange("p (c u o) -> p c o u", c=2, u=2, o=P),
                )
            grp[i] = gt

        def quant_pair(i):
            wc = codp.tile([P, 512], U32, name="wc%d" % i, tag="wc", align_bytes=64)
            ws = codp.tile([P, 512], U8, name="ws%d" % i, tag="ws", align_bytes=64)
            nc.vector.quantize_mx(out=wc[:].bitcast(FP8X4), scales=ws[:], in_=grp[i][:])
            for n, (m, g, j, off) in enumerate(pairs[i]):
                codes[(g, j)] = (wc, ws, n)

        def multiply(pr, j):
            po = pos.tile([P, 512], F32, name="po%d_%d" % (pr, j), tag="po")
            for q in range(4):
                g = 4 * pr + q
                wc, ws, n = codes[(g, j)]
                for c in range(2):
                    wl = (2 * n + c) * P
                    xl = (16 * c + g) * P
                    nc.tensor.matmul_mx(
                        out=po[:, q * P : (q + 1) * P],
                        lhsT=wc[:, wl : wl + P].bitcast(FP8X4),
                        lhsT_scale=ws[:, wl : wl + P],
                        rhs=xc[:, xl : xl + P].bitcast(FP8X4),
                        rhs_scale=xs[:, xl : xl + P],
                        start=(c == 0),
                        stop=(c == 1),
                    )
            return po

        def add_bias(pr, j, po):
            lo = 16 * j + 4 * pr
            nc.vector.tensor_tensor(
                out=ot[j][:].rearrange("p (a r n) -> p r a n", a=16, r=4, n=32)[:, pr].rearrange("p a (w q) -> p a w q", q=4),
                in0=po[:].rearrange("p (q a w) -> p a w q", q=4, a=16, w=8),
                in1=bias[:, lo : lo + 4].unsqueeze(1).unsqueeze(1).to_broadcast([P, 16, 8, 4]),
                op=mybir.AluOpType.add,
            )
            done[j] += 1
            if done[j] == 4:
                nc.sync.dma_start(
                    out=out.rearrange("b (q j) h w -> j q b (h w)", j=6)[j],
                    in_=ot[j][:].rearrange("p (b n) -> p b n", b=2),
                )

        done = [0] * 6
        x_stage()
        next_m = 0
        pending = []
        for i in range(n_pairs + LOOK + 1):
            while next_m < len(tiles) and (next_m < RAW_BUFS or last_pair[next_m - RAW_BUFS] < i):
                load_w(next_m)
                next_m += 1
            if i == 8:
                spread_bias()
            if i < n_pairs:
                transpose_pair(i)
            k = i - LOOK
            if 0 <= k < n_pairs:
                quant_pair(k)
            for pr, j, po in pending:
                add_bias(pr, j, po)
            pending = []
            if 0 <= k < n_pairs:
                for pr, j in sched[k]:
                    pending.append((pr, j, multiply(pr, j)))
